import numpy as np
import ml_dtypes

BF16 = ml_dtypes.bfloat16


def bf(x):
    return np.asarray(x, np.float32).astype(BF16)


def f32(x):
    return np.asarray(x, np.float32)


def f64(x):
    return np.asarray(x).astype(np.float64)


def striped(idx):
    return np.tile(idx.reshape(-1, 16).T, (8, 1))


C, S, R, K, P, H, N = 256, 256, 4, 5, 256, 128, 1024
SCORE_B = 0.25


def unit_cols(v):
    return v / np.sqrt((v * v).sum(axis=0, keepdims=True))


def setup_inputs():
    return {
        "x": f32(unit_cols(np.random.standard_normal((C, S)))),
        "p": f32(unit_cols(np.random.standard_normal((C, P)))),
        "w_p": f32(0.5 * np.random.standard_normal((C, 1))),
        "w_n": f32(0.5 * np.random.standard_normal((C, K))),
        "w_c": f32(4.0 * np.random.standard_normal((C, K))),
        "nbr_w": f32(np.tile(0.5 + np.random.random((1, N)), (C, 1))),
        "offs": striped(np.concatenate([np.random.permutation(S)[:H] for _ in range(N // H)])),
    }


def reference(x, p, w_p, w_n, w_c, nbr_w, offs):
    idx = offs[:16].T.reshape(-1)
    xs = f64(x)
    t = xs[:, idx] * f64(nbr_w)
    feats = np.concatenate([xs, t], axis=1).reshape(C, K, S)
    cross = (feats * f64(w_c)[:, :, None]).sum(axis=1)
    nodew = (feats * f64(w_n)[:, :, None]).sum(axis=1)
    return f64(p).T @ (cross + f64(w_p)) + nodew.sum(axis=0)[None, :] + SCORE_B

@@ -1,0 +1,103 @@
+import concourse.mybir as mybir
+
+F32 = mybir.dt.float32
+BF16 = mybir.dt.bfloat16
+U16 = mybir.dt.uint16
+MULT = mybir.AluOpType.mult
+ADD = mybir.AluOpType.add
+IDENTITY = mybir.ActivationFunctionType.Identity
+COPY = mybir.ActivationFunctionType.Copy
+
+P = 128
+C = 256
+S = 256
+PHRASES = 256
+R = 4
+N = R * S
+C_BLOCKS = C // P
+PHRASE_BLOCKS = PHRASES // P
+OFFSET_COLUMNS = S // 16
+SCORE_B = 0.25
+
+FLOPS = 2 * C * S * (PHRASES + 1)
+
+
+def tile_encodingmodel_kernel(tc, x, p, w_p, w_n, w_c, nbr_w, offs, out):
+    nc = tc.nc
+    with (
+        tc.tile_pool(name="held", bufs=1) as held,
+        tc.psum_pool(name="psum", bufs=1) as psum,
+    ):
+        offsets = held.tile([P, N // 16], U16, name="offsets")
+        nc.sync.dma_start(offsets[:], offs)
+
+        wc = held.tile([P, C_BLOCKS, R + 1], F32, name="wc")
+        wn = held.tile([P, C_BLOCKS, R + 1], F32, name="wn")
+        wp = held.tile([P, C_BLOCKS, 1], F32, name="wp")
+        nc.scalar.dma_start(wc[:], w_c.rearrange("(b c) k -> c b k", c=P))
+        nc.scalar.dma_start(wn[:], w_n.rearrange("(b c) k -> c b k", c=P))
+        nc.scalar.dma_start(wp[:], w_p.rearrange("(b c) k -> c b k", c=P))
+
+        x_blocks = []
+        mask_blocks = []
+        for b in range(C_BLOCKS):
+            rows = slice(b * P, (b + 1) * P)
+            x_b = held.tile([P, S], F32, name=f"x{b}")
+            nc.sync.dma_start(x_b[:], x[rows, :])
+            x_blocks.append(x_b)
+            block_masks = []
+            for r in range(R):
+                mask = held.tile([P, S], F32, name=f"mask{b}_{r}")
+                queue = nc.scalar if r % 2 == 0 else nc.sync
+                queue.dma_start(mask[:], nbr_w[rows, r * S : (r + 1) * S])
+                block_masks.append(mask)
+            mask_blocks.append(block_masks)
+
+        p_blocks = []
+        for b in range(C_BLOCKS):
+            p_f32 = held.tile([P, PHRASES], F32, name=f"p_f32_{b}")
+            queue = nc.scalar if b % 2 == 0 else nc.sync
+            queue.dma_start(p_f32[:], p[b * P : (b + 1) * P, :])
+            p_blocks.append(p_f32)
+
+        ones = held.tile([P, P], BF16, name="ones")
+        nc.gpsimd.memset(ones[:], 1.0)
+
+        scores = [psum.tile([P, S], F32, name=f"scores{i}") for i in range(PHRASE_BLOCKS)]
+
+        for b in range(C_BLOCKS):
+            x_b = x_blocks[b]
+
+            cross = held.tile([P, S], F32, name=f"cross{b}_0")
+            nodew = held.tile([P, S], F32, name=f"nodew{b}_0")
+            nc.scalar.activation(cross[:], x_b[:], IDENTITY, bias=wp[:, b, :], scale=wc[:, b, 0:1])
+            nc.scalar.activation(nodew[:], x_b[:], COPY, scale=wn[:, b, 0:1])
+
+            p_bf = held.tile([P, PHRASES], BF16, name=f"p_bf{b}")
+            nc.scalar.copy(p_bf[:], p_blocks[b][:])
+
+            for r in range(1, R + 1):
+                t = held.tile([P, S], F32, name=f"t{b}_{r}")
+                neighbour = offsets[:, (r - 1) * OFFSET_COLUMNS : r * OFFSET_COLUMNS]
+                nc.vector.tensor_tensor(t[:], x_b[:].indirect(neighbour), mask_blocks[b][r - 1][:], MULT)
+
+                sum_dt = BF16 if r == R else F32
+                cross_next = held.tile([P, S], sum_dt, name=f"cross{b}_{r}")
+                nodew_next = held.tile([P, S], sum_dt, name=f"nodew{b}_{r}")
+                nc.vector.scalar_tensor_tensor(cross_next[:], t[:], wc[:, b, r : r + 1], cross[:], MULT, ADD)
+                nc.vector.scalar_tensor_tensor(nodew_next[:], t[:], wn[:, b, r : r + 1], nodew[:], MULT, ADD)
+                cross, nodew = cross_next, nodew_next
+
+            for i in range(PHRASE_BLOCKS):
+                nc.tensor.matmul(scores[i][:], p_bf[:, i * P : (i + 1) * P], cross[:], start=(b == 0), stop=False)
+            for i in range(PHRASE_BLOCKS):
+                nc.tensor.matmul(scores[i][:], ones[:], nodew[:], start=False, stop=(b == C_BLOCKS - 1))
+
+        for i in range(PHRASE_BLOCKS):
+            result = held.tile([P, S], F32, name=f"result{i}")
+            if i % 2 == 0:
+                nc.vector.tensor_scalar_add(result[:], scores[i][:], SCORE_B)
+                nc.sync.dma_start(out[i * P : (i + 1) * P, :], result[:])
+            else:
+                nc.scalar.activation(result[:], scores[i][:], COPY, bias=SCORE_B)
+                nc.scalar.dma_start(out[i * P : (i + 1) * P, :], result[:])

@@ -1,4 +1,5 @@
 import concourse.mybir as mybir
+from concourse.masks import make_identity
 
 F32 = mybir.dt.float32
 BF16 = mybir.dt.bfloat16
@@ -63,35 +64,62 @@ def tile_encodingmodel_kernel(tc, x, p, w_p, w_n, w_c, nbr_w, offs, out):
         ones = held.tile([P, P], BF16, name="ones")
         nc.gpsimd.memset(ones[:], 1.0)
 
+        identity = held.tile([P, P], F32, name="identity")
+        make_identity(nc, identity[:])
+
         scores = [psum.tile([P, S], F32, name=f"scores{i}") for i in range(PHRASE_BLOCKS)]
 
+        def look_up(b, r):
+            t = held.tile([P, S], F32, name=f"t{b}_{r}")
+            neighbour = offsets[:, (r - 1) * OFFSET_COLUMNS : r * OFFSET_COLUMNS]
+            nc.vector.tensor_tensor(t[:], x_blocks[b][:].indirect(neighbour), mask_blocks[b][r - 1][:], MULT)
+            return t
+
+        def add_to_scores(b, cross_bf, nodew_bf):
+            for i in range(PHRASE_BLOCKS):
+                nc.tensor.matmul(
+                    scores[i][:], p_bf_blocks[b][:, i * P : (i + 1) * P], cross_bf[:], start=(b == 0), stop=False
+                )
+            for i in range(PHRASE_BLOCKS):
+                nc.tensor.matmul(scores[i][:], ones[:], nodew_bf[:], start=False, stop=(b == C_BLOCKS - 1))
+
+        b = 1
+        cross = held.tile([P, S], F32, name="cross_0")
+        nodew = held.tile([P, S], F32, name="nodew_0")
+        nc.scalar.activation(cross[:], x_blocks[b][:], IDENTITY, bias=wp[:, b, :], scale=wc[:, b, 0:1])
+        nc.scalar.activation(nodew[:], x_blocks[b][:], COPY, scale=wn[:, b, 0:1])
+
+        b = 0
+        cross_sum = psum.tile([P, S], F32, name="cross_sum")
+        nodew_sum = psum.tile([P, S], F32, name="nodew_sum")
+        for r in range(R + 1):
+            term = x_blocks[b] if r == 0 else look_up(b, r)
+            for total, weights, label in ((cross_sum, wc, "c"), (nodew_sum, wn, "n")):
+                product = held.tile([P, S], F32, name=f"product_{label}{r}")
+                nc.scalar.activation(product[:], term[:], COPY, scale=weights[:, b, r : r + 1])
+                nc.tensor.matmul(total[:], identity[:], product[:], start=(r == 0), stop=(r == R))
+        cross_bf = held.tile([P, S], BF16, name=f"cross_bf{b}")
+        nodew_bf = held.tile([P, S], BF16, name=f"nodew_bf{b}")
+        nc.scalar.activation(cross_bf[:], cross_sum[:], IDENTITY, bias=wp[:, b, :])
+        nc.scalar.copy(nodew_bf[:], nodew_sum[:])
+
+        p_bf_blocks = []
         for b in range(C_BLOCKS):
-            x_b = x_blocks[b]
-
-            cross = held.tile([P, S], F32, name=f"cross{b}_0")
-            nodew = held.tile([P, S], F32, name=f"nodew{b}_0")
-            nc.scalar.activation(cross[:], x_b[:], IDENTITY, bias=wp[:, b, :], scale=wc[:, b, 0:1])
-            nc.scalar.activation(nodew[:], x_b[:], COPY, scale=wn[:, b, 0:1])
-
             p_bf = held.tile([P, PHRASES], BF16, name=f"p_bf{b}")
             nc.scalar.copy(p_bf[:], p_blocks[b][:])
+            p_bf_blocks.append(p_bf)
+        add_to_scores(0, cross_bf, nodew_bf)
 
-            for r in range(1, R + 1):
-                t = held.tile([P, S], F32, name=f"t{b}_{r}")
-                neighbour = offsets[:, (r - 1) * OFFSET_COLUMNS : r * OFFSET_COLUMNS]
-                nc.vector.tensor_tensor(t[:], x_b[:].indirect(neighbour), mask_blocks[b][r - 1][:], MULT)
-
-                sum_dt = BF16 if r == R else F32
-                cross_next = held.tile([P, S], sum_dt, name=f"cross{b}_{r}")
-                nodew_next = held.tile([P, S], sum_dt, name=f"nodew{b}_{r}")
-                nc.vector.scalar_tensor_tensor(cross_next[:], t[:], wc[:, b, r : r + 1], cross[:], MULT, ADD)
-                nc.vector.scalar_tensor_tensor(nodew_next[:], t[:], wn[:, b, r : r + 1], nodew[:], MULT, ADD)
-                cross, nodew = cross_next, nodew_next
-
-            for i in range(PHRASE_BLOCKS):
-                nc.tensor.matmul(scores[i][:], p_bf[:, i * P : (i + 1) * P], cross[:], start=(b == 0), stop=False)
-            for i in range(PHRASE_BLOCKS):
-                nc.tensor.matmul(scores[i][:], ones[:], nodew[:], start=False, stop=(b == C_BLOCKS - 1))
+        b = 1
+        for r in range(1, R + 1):
+            t = look_up(b, r)
+            sum_dt = BF16 if r == R else F32
+            cross_next = held.tile([P, S], sum_dt, name=f"cross_{r}")
+            nodew_next = held.tile([P, S], sum_dt, name=f"nodew_{r}")
+            nc.vector.scalar_tensor_tensor(cross_next[:], t[:], wc[:, b, r : r + 1], cross[:], MULT, ADD)
+            nc.vector.scalar_tensor_tensor(nodew_next[:], t[:], wn[:, b, r : r + 1], nodew[:], MULT, ADD)
+            cross, nodew = cross_next, nodew_next
+        add_to_scores(b, cross, nodew)
 
         for i in range(PHRASE_BLOCKS):
             result = held.tile([P, S], F32, name=f"result{i}")

@@ -1,5 +1,4 @@
 import concourse.mybir as mybir
-from concourse.masks import make_identity
 
 F32 = mybir.dt.float32
 BF16 = mybir.dt.bfloat16
@@ -64,10 +63,22 @@ def tile_encodingmodel_kernel(tc, x, p, w_p, w_n, w_c, nbr_w, offs, out):
         ones = held.tile([P, P], BF16, name="ones")
         nc.gpsimd.memset(ones[:], 1.0)
 
-        identity = held.tile([P, P], F32, name="identity")
-        make_identity(nc, identity[:])
-
         scores = [psum.tile([P, S], F32, name=f"scores{i}") for i in range(PHRASE_BLOCKS)]
+
+        cross = []
+        nodew = []
+        p_bf_blocks = []
+        for b in range(C_BLOCKS):
+            cross_b = held.tile([P, S], F32, name=f"cross{b}_0")
+            nodew_b = held.tile([P, S], F32, name=f"nodew{b}_0")
+            nc.scalar.activation(cross_b[:], x_blocks[b][:], IDENTITY, bias=wp[:, b, :], scale=wc[:, b, 0:1])
+            nc.scalar.activation(nodew_b[:], x_blocks[b][:], COPY, scale=wn[:, b, 0:1])
+            cross.append(cross_b)
+            nodew.append(nodew_b)
+        for b in range(C_BLOCKS):
+            p_bf = held.tile([P, PHRASES], BF16, name=f"p_bf{b}")
+            nc.scalar.copy(p_bf[:], p_blocks[b][:])
+            p_bf_blocks.append(p_bf)
 
         def look_up(b, r):
             t = held.tile([P, S], F32, name=f"t{b}_{r}")
@@ -75,51 +86,32 @@ def tile_encodingmodel_kernel(tc, x, p, w_p, w_n, w_c, nbr_w, offs, out):
             nc.vector.tensor_tensor(t[:], x_blocks[b][:].indirect(neighbour), mask_blocks[b][r - 1][:], MULT)
             return t
 
-        def add_to_scores(b, cross_bf, nodew_bf):
+        def add_to_sums(b, r, t):
+            sum_dt = BF16 if r == R else F32
+            cross_next = held.tile([P, S], sum_dt, name=f"cross{b}_{r}")
+            nodew_next = held.tile([P, S], sum_dt, name=f"nodew{b}_{r}")
+            nc.vector.scalar_tensor_tensor(cross_next[:], t[:], wc[:, b, r : r + 1], cross[b][:], MULT, ADD)
+            nc.vector.scalar_tensor_tensor(nodew_next[:], t[:], wn[:, b, r : r + 1], nodew[b][:], MULT, ADD)
+            cross[b] = cross_next
+            nodew[b] = nodew_next
+
+        def add_to_scores(b):
             for i in range(PHRASE_BLOCKS):
                 nc.tensor.matmul(
-                    scores[i][:], p_bf_blocks[b][:, i * P : (i + 1) * P], cross_bf[:], start=(b == 0), stop=False
+                    scores[i][:], p_bf_blocks[b][:, i * P : (i + 1) * P], cross[b][:], start=(b == 0), stop=False
                 )
             for i in range(PHRASE_BLOCKS):
-                nc.tensor.matmul(scores[i][:], ones[:], nodew_bf[:], start=False, stop=(b == C_BLOCKS - 1))
+                nc.tensor.matmul(scores[i][:], ones[:], nodew[b][:], start=False, stop=(b == C_BLOCKS - 1))
 
-        b = 1
-        cross = held.tile([P, S], F32, name="cross_0")
-        nodew = held.tile([P, S], F32, name="nodew_0")
-        nc.scalar.activation(cross[:], x_blocks[b][:], IDENTITY, bias=wp[:, b, :], scale=wc[:, b, 0:1])
-        nc.scalar.activation(nodew[:], x_blocks[b][:], COPY, scale=wn[:, b, 0:1])
-
-        b = 0
-        cross_sum = psum.tile([P, S], F32, name="cross_sum")
-        nodew_sum = psum.tile([P, S], F32, name="nodew_sum")
-        for r in range(R + 1):
-            term = x_blocks[b] if r == 0 else look_up(b, r)
-            for total, weights, label in ((cross_sum, wc, "c"), (nodew_sum, wn, "n")):
-                product = held.tile([P, S], F32, name=f"product_{label}{r}")
-                nc.scalar.activation(product[:], term[:], COPY, scale=weights[:, b, r : r + 1])
-                nc.tensor.matmul(total[:], identity[:], product[:], start=(r == 0), stop=(r == R))
-        cross_bf = held.tile([P, S], BF16, name=f"cross_bf{b}")
-        nodew_bf = held.tile([P, S], BF16, name=f"nodew_bf{b}")
-        nc.scalar.activation(cross_bf[:], cross_sum[:], IDENTITY, bias=wp[:, b, :])
-        nc.scalar.copy(nodew_bf[:], nodew_sum[:])
-
-        p_bf_blocks = []
-        for b in range(C_BLOCKS):
-            p_bf = held.tile([P, PHRASES], BF16, name=f"p_bf{b}")
-            nc.scalar.copy(p_bf[:], p_blocks[b][:])
-            p_bf_blocks.append(p_bf)
-        add_to_scores(0, cross_bf, nodew_bf)
-
-        b = 1
-        for r in range(1, R + 1):
-            t = look_up(b, r)
-            sum_dt = BF16 if r == R else F32
-            cross_next = held.tile([P, S], sum_dt, name=f"cross_{r}")
-            nodew_next = held.tile([P, S], sum_dt, name=f"nodew_{r}")
-            nc.vector.scalar_tensor_tensor(cross_next[:], t[:], wc[:, b, r : r + 1], cross[:], MULT, ADD)
-            nc.vector.scalar_tensor_tensor(nodew_next[:], t[:], wn[:, b, r : r + 1], nodew[:], MULT, ADD)
-            cross, nodew = cross_next, nodew_next
-        add_to_scores(b, cross, nodew)
+        steps = [(b, r) for b in range(C_BLOCKS) for r in range(1, R + 1)]
+        looked_up = look_up(*steps[0])
+        for k, (b, r) in enumerate(steps):
+            t = looked_up
+            if k + 1 < len(steps):
+                looked_up = look_up(*steps[k + 1])
+            add_to_sums(b, r, t)
+            if r == R:
+                add_to_scores(b)
 
         for i in range(PHRASE_BLOCKS):
             result = held.tile([P, S], F32, name=f"result{i}")

@@ -1,4 +1,5 @@
 import concourse.mybir as mybir
+from concourse.masks import make_identity
 
 F32 = mybir.dt.float32
 BF16 = mybir.dt.bfloat16
@@ -40,6 +41,7 @@ def tile_encodingmodel_kernel(tc, x, p, w_p, w_n, w_c, nbr_w, offs, out):
 
         x_blocks = []
         mask_blocks = []
+        p_blocks = []
         for b in range(C_BLOCKS):
             rows = slice(b * P, (b + 1) * P)
             x_b = held.tile([P, S], F32, name=f"x{b}")
@@ -52,66 +54,58 @@ def tile_encodingmodel_kernel(tc, x, p, w_p, w_n, w_c, nbr_w, offs, out):
                 queue.dma_start(mask[:], nbr_w[rows, r * S : (r + 1) * S])
                 block_masks.append(mask)
             mask_blocks.append(block_masks)
-
-        p_blocks = []
-        for b in range(C_BLOCKS):
-            p_f32 = held.tile([P, PHRASES], F32, name=f"p_f32_{b}")
-            queue = nc.scalar if b % 2 == 0 else nc.sync
-            queue.dma_start(p_f32[:], p[b * P : (b + 1) * P, :])
-            p_blocks.append(p_f32)
+            if b == 0:
+                for pb in range(C_BLOCKS):
+                    p_f32 = held.tile([P, PHRASES], F32, name=f"p_f32_{pb}")
+                    queue = nc.scalar if pb % 2 == 0 else nc.sync
+                    queue.dma_start(p_f32[:], p[pb * P : (pb + 1) * P, :])
+                    p_blocks.append(p_f32)
 
         ones = held.tile([P, P], BF16, name="ones")
         nc.gpsimd.memset(ones[:], 1.0)
+        identity = held.tile([P, P], F32, name="identity")
+        make_identity(nc, identity[:])
 
         scores = [psum.tile([P, S], F32, name=f"scores{i}") for i in range(PHRASE_BLOCKS)]
-
-        cross = []
-        nodew = []
         p_bf_blocks = []
+
         for b in range(C_BLOCKS):
-            cross_b = held.tile([P, S], F32, name=f"cross{b}_0")
-            nodew_b = held.tile([P, S], F32, name=f"nodew{b}_0")
-            nc.scalar.activation(cross_b[:], x_blocks[b][:], IDENTITY, bias=wp[:, b, :], scale=wc[:, b, 0:1])
-            nc.scalar.activation(nodew_b[:], x_blocks[b][:], COPY, scale=wn[:, b, 0:1])
-            cross.append(cross_b)
-            nodew.append(nodew_b)
-        for b in range(C_BLOCKS):
-            p_bf = held.tile([P, PHRASES], BF16, name=f"p_bf{b}")
-            nc.scalar.copy(p_bf[:], p_blocks[b][:])
-            p_bf_blocks.append(p_bf)
+            x_b = x_blocks[b]
+            nodew = held.tile([P, S], F32, name=f"nodew{b}_0")
+            nc.scalar.activation(nodew[:], x_b[:], COPY, scale=wn[:, b, 0:1])
+            cross_sum = psum.tile([P, S], F32, name=f"cross_sum{b}")
+            product = held.tile([P, S], F32, name=f"product{b}_0")
+            nc.scalar.activation(product[:], x_b[:], IDENTITY, bias=wp[:, b, :], scale=wc[:, b, 0:1])
+            nc.tensor.matmul(cross_sum[:], identity[:], product[:], start=True, stop=False)
 
-        def look_up(b, r):
-            t = held.tile([P, S], F32, name=f"t{b}_{r}")
-            neighbour = offsets[:, (r - 1) * OFFSET_COLUMNS : r * OFFSET_COLUMNS]
-            nc.vector.tensor_tensor(t[:], x_blocks[b][:].indirect(neighbour), mask_blocks[b][r - 1][:], MULT)
-            return t
+            for r in range(1, R + 1):
+                t = held.tile([P, S], F32, name=f"t{b}_{r}")
+                neighbour = offsets[:, (r - 1) * OFFSET_COLUMNS : r * OFFSET_COLUMNS]
+                nc.vector.tensor_tensor(t[:], x_b[:].indirect(neighbour), mask_blocks[b][r - 1][:], MULT)
 
-        def add_to_sums(b, r, t):
-            sum_dt = BF16 if r == R else F32
-            cross_next = held.tile([P, S], sum_dt, name=f"cross{b}_{r}")
-            nodew_next = held.tile([P, S], sum_dt, name=f"nodew{b}_{r}")
-            nc.vector.scalar_tensor_tensor(cross_next[:], t[:], wc[:, b, r : r + 1], cross[b][:], MULT, ADD)
-            nc.vector.scalar_tensor_tensor(nodew_next[:], t[:], wn[:, b, r : r + 1], nodew[b][:], MULT, ADD)
-            cross[b] = cross_next
-            nodew[b] = nodew_next
+                nodew_next = held.tile([P, S], BF16 if r == R else F32, name=f"nodew{b}_{r}")
+                nc.vector.scalar_tensor_tensor(nodew_next[:], t[:], wn[:, b, r : r + 1], nodew[:], MULT, ADD)
+                nodew = nodew_next
+                if r < R:
+                    product = held.tile([P, S], F32, name=f"product{b}_{r}")
+                    nc.scalar.activation(product[:], t[:], COPY, scale=wc[:, b, r : r + 1])
+                    nc.tensor.matmul(cross_sum[:], identity[:], product[:], start=False, stop=(r == R - 1))
+                else:
+                    cross = held.tile([P, S], BF16, name=f"cross{b}")
+                    nc.vector.scalar_tensor_tensor(cross[:], t[:], wc[:, b, r : r + 1], cross_sum[:], MULT, ADD)
 
-        def add_to_scores(b):
+            if b == 0:
+                for pb in range(C_BLOCKS):
+                    p_bf = held.tile([P, PHRASES], BF16, name=f"p_bf{pb}")
+                    nc.scalar.copy(p_bf[:], p_blocks[pb][:])
+                    p_bf_blocks.append(p_bf)
+
+            for i in range(PHRASE_BLOCKS):
+                nc.tensor.matmul(scores[i][:], ones[:], nodew[:], start=(b == 0), stop=False)
             for i in range(PHRASE_BLOCKS):
                 nc.tensor.matmul(
-                    scores[i][:], p_bf_blocks[b][:, i * P : (i + 1) * P], cross[b][:], start=(b == 0), stop=False
+                    scores[i][:], p_bf_blocks[b][:, i * P : (i + 1) * P], cross[:], start=False, stop=(b == C_BLOCKS - 1)
                 )
-            for i in range(PHRASE_BLOCKS):
-                nc.tensor.matmul(scores[i][:], ones[:], nodew[b][:], start=False, stop=(b == C_BLOCKS - 1))
-
-        steps = [(b, r) for b in range(C_BLOCKS) for r in range(1, R + 1)]
-        looked_up = look_up(*steps[0])
-        for k, (b, r) in enumerate(steps):
-            t = looked_up
-            if k + 1 < len(steps):
-                looked_up = look_up(*steps[k + 1])
-            add_to_sums(b, r, t)
-            if r == R:
-                add_to_scores(b)
 
         for i in range(PHRASE_BLOCKS):
             result = held.tile([P, S], F32, name=f"result{i}")

@@ -32,79 +32,76 @@ def tile_encodingmodel_kernel(tc, x, p, w_p, w_n, w_c, nbr_w, offs, out):
         offsets = held.tile([P, N // 16], U16, name="offsets")
         nc.sync.dma_start(offsets[:], offs)
 
-        wc = held.tile([P, C_BLOCKS, R + 1], F32, name="wc")
-        wn = held.tile([P, C_BLOCKS, R + 1], F32, name="wn")
-        wp = held.tile([P, C_BLOCKS, 1], F32, name="wp")
-        nc.scalar.dma_start(wc[:], w_c.rearrange("(b c) k -> c b k", c=P))
-        nc.scalar.dma_start(wn[:], w_n.rearrange("(b c) k -> c b k", c=P))
-        nc.scalar.dma_start(wp[:], w_p.rearrange("(b c) k -> c b k", c=P))
-
         x_blocks = []
         mask_blocks = []
-        p_blocks = []
         for b in range(C_BLOCKS):
             rows = slice(b * P, (b + 1) * P)
             x_b = held.tile([P, S], F32, name=f"x{b}")
             nc.sync.dma_start(x_b[:], x[rows, :])
             x_blocks.append(x_b)
-            block_masks = []
-            for r in range(R):
-                mask = held.tile([P, S], F32, name=f"mask{b}_{r}")
-                queue = nc.scalar if r % 2 == 0 else nc.sync
-                queue.dma_start(mask[:], nbr_w[rows, r * S : (r + 1) * S])
-                block_masks.append(mask)
-            mask_blocks.append(block_masks)
+            mask_b = held.tile([P, N], F32, name=f"mask{b}")
+            nc.sync.dma_start(mask_b[:, 0:S], nbr_w[rows, 0:S])
+            mask_blocks.append(mask_b)
             if b == 0:
-                for pb in range(C_BLOCKS):
-                    p_f32 = held.tile([P, PHRASES], F32, name=f"p_f32_{pb}")
-                    queue = nc.scalar if pb % 2 == 0 else nc.sync
-                    queue.dma_start(p_f32[:], p[pb * P : (pb + 1) * P, :])
-                    p_blocks.append(p_f32)
+                wc = held.tile([P, C_BLOCKS, R + 1], F32, name="wc")
+                wn = held.tile([P, C_BLOCKS, R + 1], F32, name="wn")
+                wp = held.tile([P, C_BLOCKS, 1], F32, name="wp")
+                nc.sync.dma_start(wn[:], w_n.rearrange("(b c) k -> c b k", c=P))
+                nc.sync.dma_start(wc[:], w_c.rearrange("(b c) k -> c b k", c=P))
+                nc.sync.dma_start(wp[:], w_p.rearrange("(b c) k -> c b k", c=P))
+        for b in range(C_BLOCKS):
+            nc.sync.dma_start(mask_blocks[b][:, S:N], nbr_w[b * P : (b + 1) * P, S:N])
+        p_f32 = held.tile([P, C_BLOCKS, PHRASES], F32, name="p_f32")
+        nc.sync.dma_start(p_f32[:], p.rearrange("(b c) i -> c b i", c=P))
 
+        ones_f32 = held.tile([P, P], F32, name="ones_f32")
+        nc.gpsimd.memset(ones_f32[:], 1.0)
         ones = held.tile([P, P], BF16, name="ones")
-        nc.gpsimd.memset(ones[:], 1.0)
+        nc.scalar.copy(ones[:], ones_f32[:])
         identity = held.tile([P, P], F32, name="identity")
         make_identity(nc, identity[:])
 
-        scores = [psum.tile([P, S], F32, name=f"scores{i}") for i in range(PHRASE_BLOCKS)]
-        p_bf_blocks = []
-
+        nodew = []
+        cross_sums = []
         for b in range(C_BLOCKS):
-            x_b = x_blocks[b]
-            nodew = held.tile([P, S], F32, name=f"nodew{b}_0")
-            nc.scalar.activation(nodew[:], x_b[:], COPY, scale=wn[:, b, 0:1])
+            nodew_b = held.tile([P, S], F32, name=f"nodew{b}_0")
+            nc.scalar.activation(nodew_b[:], x_blocks[b][:], COPY, scale=wn[:, b, 0:1])
+            nodew.append(nodew_b)
             cross_sum = psum.tile([P, S], F32, name=f"cross_sum{b}")
             product = held.tile([P, S], F32, name=f"product{b}_0")
-            nc.scalar.activation(product[:], x_b[:], IDENTITY, bias=wp[:, b, :], scale=wc[:, b, 0:1])
+            nc.scalar.activation(product[:], x_blocks[b][:], IDENTITY, bias=wp[:, b, :], scale=wc[:, b, 0:1])
             nc.tensor.matmul(cross_sum[:], identity[:], product[:], start=True, stop=False)
+            cross_sums.append(cross_sum)
 
-            for r in range(1, R + 1):
+        last_t = []
+        for r in range(1, R + 1):
+            for b in range(C_BLOCKS):
                 t = held.tile([P, S], F32, name=f"t{b}_{r}")
                 neighbour = offsets[:, (r - 1) * OFFSET_COLUMNS : r * OFFSET_COLUMNS]
-                nc.vector.tensor_tensor(t[:], x_b[:].indirect(neighbour), mask_blocks[b][r - 1][:], MULT)
+                nc.vector.tensor_tensor(t[:], x_blocks[b][:].indirect(neighbour), mask_blocks[b][:, (r - 1) * S : r * S], MULT)
 
                 nodew_next = held.tile([P, S], BF16 if r == R else F32, name=f"nodew{b}_{r}")
-                nc.vector.scalar_tensor_tensor(nodew_next[:], t[:], wn[:, b, r : r + 1], nodew[:], MULT, ADD)
-                nodew = nodew_next
+                nc.vector.scalar_tensor_tensor(nodew_next[:], t[:], wn[:, b, r : r + 1], nodew[b][:], MULT, ADD)
+                nodew[b] = nodew_next
                 if r < R:
                     product = held.tile([P, S], F32, name=f"product{b}_{r}")
                     nc.scalar.activation(product[:], t[:], COPY, scale=wc[:, b, r : r + 1])
-                    nc.tensor.matmul(cross_sum[:], identity[:], product[:], start=False, stop=(r == R - 1))
+                    nc.tensor.matmul(cross_sums[b][:], identity[:], product[:], start=False, stop=(r == R - 1))
                 else:
-                    cross = held.tile([P, S], BF16, name=f"cross{b}")
-                    nc.vector.scalar_tensor_tensor(cross[:], t[:], wc[:, b, r : r + 1], cross_sum[:], MULT, ADD)
+                    last_t.append(t)
 
-            if b == 0:
-                for pb in range(C_BLOCKS):
-                    p_bf = held.tile([P, PHRASES], BF16, name=f"p_bf{pb}")
-                    nc.scalar.copy(p_bf[:], p_blocks[pb][:])
-                    p_bf_blocks.append(p_bf)
-
+        scores = [psum.tile([P, S], F32, name=f"scores{i}") for i in range(PHRASE_BLOCKS)]
+        for b in range(C_BLOCKS):
             for i in range(PHRASE_BLOCKS):
-                nc.tensor.matmul(scores[i][:], ones[:], nodew[:], start=(b == 0), stop=False)
+                nc.tensor.matmul(scores[i][:], ones[:], nodew[b][:], start=(b == 0), stop=False)
+        for b in range(C_BLOCKS):
+            p_bf = held.tile([P, PHRASES], BF16, name=f"p_bf{b}")
+            nc.scalar.copy(p_bf[:], p_f32[:, b, :])
+            cross = held.tile([P, S], BF16, name=f"cross{b}")
+            nc.vector.scalar_tensor_tensor(cross[:], last_t[b][:], wc[:, b, R : R + 1], cross_sums[b][:], MULT, ADD)
             for i in range(PHRASE_BLOCKS):
                 nc.tensor.matmul(
-                    scores[i][:], p_bf_blocks[b][:, i * P : (i + 1) * P], cross[:], start=False, stop=(b == C_BLOCKS - 1)
+                    scores[i][:], p_bf[:, i * P : (i + 1) * P], cross[:], start=False, stop=(b == C_BLOCKS - 1)
                 )
 
         for i in range(PHRASE_BLOCKS):

@@ -19,6 +19,7 @@ C_BLOCKS = C // P
 PHRASE_BLOCKS = PHRASES // P
 OFFSET_COLUMNS = S // 16
 SCORE_B = 0.25
+WARM_UP_MATMULS = 8
 
 FLOPS = 2 * C * S * (PHRASES + 1)
 
@@ -60,6 +61,10 @@ def tile_encodingmodel_kernel(tc, x, p, w_p, w_n, w_c, nbr_w, offs, out):
         nc.scalar.copy(ones[:], ones_f32[:])
         identity = held.tile([P, P], F32, name="identity")
         make_identity(nc, identity[:])
+
+        warm_up = psum.tile([P, P], F32, name="warm_up")
+        for k in range(WARM_UP_MATMULS):
+            nc.tensor.matmul(warm_up[:], identity[:], identity[:], start=True, stop=True)
 
         nodew = []
         cross_sums = []

@@ -1,5 +1,4 @@
 import concourse.mybir as mybir
-from concourse.masks import make_identity
 
 F32 = mybir.dt.float32
 BF16 = mybir.dt.bfloat16
@@ -19,7 +18,6 @@ C_BLOCKS = C // P
 PHRASE_BLOCKS = PHRASES // P
 OFFSET_COLUMNS = S // 16
 SCORE_B = 0.25
-WARM_UP_MATMULS = 8
 
 FLOPS = 2 * C * S * (PHRASES + 1)
 
@@ -59,55 +57,38 @@ def tile_encodingmodel_kernel(tc, x, p, w_p, w_n, w_c, nbr_w, offs, out):
         nc.gpsimd.memset(ones_f32[:], 1.0)
         ones = held.tile([P, P], BF16, name="ones")
         nc.scalar.copy(ones[:], ones_f32[:])
-        identity = held.tile([P, P], F32, name="identity")
-        make_identity(nc, identity[:])
-
-        warm_up = psum.tile([P, P], F32, name="warm_up")
-        for k in range(WARM_UP_MATMULS):
-            nc.tensor.matmul(warm_up[:], identity[:], identity[:], start=True, stop=True)
-
+        cross = []
         nodew = []
-        cross_sums = []
         for b in range(C_BLOCKS):
+            cross_b = held.tile([P, S], F32, name=f"cross{b}_0")
             nodew_b = held.tile([P, S], F32, name=f"nodew{b}_0")
+            nc.scalar.activation(cross_b[:], x_blocks[b][:], IDENTITY, bias=wp[:, b, :], scale=wc[:, b, 0:1])
             nc.scalar.activation(nodew_b[:], x_blocks[b][:], COPY, scale=wn[:, b, 0:1])
+            cross.append(cross_b)
             nodew.append(nodew_b)
-            cross_sum = psum.tile([P, S], F32, name=f"cross_sum{b}")
-            product = held.tile([P, S], F32, name=f"product{b}_0")
-            nc.scalar.activation(product[:], x_blocks[b][:], IDENTITY, bias=wp[:, b, :], scale=wc[:, b, 0:1])
-            nc.tensor.matmul(cross_sum[:], identity[:], product[:], start=True, stop=False)
-            cross_sums.append(cross_sum)
 
-        last_t = []
         for r in range(1, R + 1):
             for b in range(C_BLOCKS):
                 t = held.tile([P, S], F32, name=f"t{b}_{r}")
                 neighbour = offsets[:, (r - 1) * OFFSET_COLUMNS : r * OFFSET_COLUMNS]
                 nc.vector.tensor_tensor(t[:], x_blocks[b][:].indirect(neighbour), mask_blocks[b][:, (r - 1) * S : r * S], MULT)
 
-                nodew_next = held.tile([P, S], BF16 if r == R else F32, name=f"nodew{b}_{r}")
+                sum_dt = BF16 if r == R else F32
+                cross_next = held.tile([P, S], sum_dt, name=f"cross{b}_{r}")
+                nodew_next = held.tile([P, S], sum_dt, name=f"nodew{b}_{r}")
+                nc.vector.scalar_tensor_tensor(cross_next[:], t[:], wc[:, b, r : r + 1], cross[b][:], MULT, ADD)
                 nc.vector.scalar_tensor_tensor(nodew_next[:], t[:], wn[:, b, r : r + 1], nodew[b][:], MULT, ADD)
+                cross[b] = cross_next
                 nodew[b] = nodew_next
-                if r < R:
-                    product = held.tile([P, S], F32, name=f"product{b}_{r}")
-                    nc.scalar.activation(product[:], t[:], COPY, scale=wc[:, b, r : r + 1])
-                    nc.tensor.matmul(cross_sums[b][:], identity[:], product[:], start=False, stop=(r == R - 1))
-                else:
-                    last_t.append(t)
 
         scores = [psum.tile([P, S], F32, name=f"scores{i}") for i in range(PHRASE_BLOCKS)]
         for b in range(C_BLOCKS):
-            for i in range(PHRASE_BLOCKS):
-                nc.tensor.matmul(scores[i][:], ones[:], nodew[b][:], start=(b == 0), stop=False)
-        for b in range(C_BLOCKS):
             p_bf = held.tile([P, PHRASES], BF16, name=f"p_bf{b}")
             nc.scalar.copy(p_bf[:], p_f32[:, b, :])
-            cross = held.tile([P, S], BF16, name=f"cross{b}")
-            nc.vector.scalar_tensor_tensor(cross[:], last_t[b][:], wc[:, b, R : R + 1], cross_sums[b][:], MULT, ADD)
             for i in range(PHRASE_BLOCKS):
-                nc.tensor.matmul(
-                    scores[i][:], p_bf[:, i * P : (i + 1) * P], cross[:], start=False, stop=(b == C_BLOCKS - 1)
-                )
+                nc.tensor.matmul(scores[i][:], p_bf[:, i * P : (i + 1) * P], cross[b][:], start=(b == 0), stop=False)
+            for i in range(PHRASE_BLOCKS):
+                nc.tensor.matmul(scores[i][:], ones[:], nodew[b][:], start=False, stop=(b == C_BLOCKS - 1))
 
         for i in range(PHRASE_BLOCKS):
             result = held.tile([P, S], F32, name=f"result{i}")

@@ -1,4 +1,5 @@
 import concourse.mybir as mybir
+from concourse.masks import make_identity
 
 F32 = mybir.dt.float32
 BF16 = mybir.dt.bfloat16
@@ -31,64 +32,78 @@ def tile_encodingmodel_kernel(tc, x, p, w_p, w_n, w_c, nbr_w, offs, out):
         offsets = held.tile([P, N // 16], U16, name="offsets")
         nc.sync.dma_start(offsets[:], offs)
 
+        x_view = x.rearrange("(q b) s -> q b s", b=C_BLOCKS)
+        mask_view = nbr_w.rearrange("(q b) j -> q b j", b=C_BLOCKS)
         x_blocks = []
         mask_blocks = []
         for b in range(C_BLOCKS):
-            rows = slice(b * P, (b + 1) * P)
             x_b = held.tile([P, S], F32, name=f"x{b}")
-            nc.sync.dma_start(x_b[:], x[rows, :])
+            nc.sync.dma_start(x_b[:], x_view[:, b, :])
             x_blocks.append(x_b)
             mask_b = held.tile([P, N], F32, name=f"mask{b}")
-            nc.sync.dma_start(mask_b[:, 0:S], nbr_w[rows, 0:S])
+            nc.sync.dma_start(mask_b[:, 0:S], mask_view[:, b, 0:S])
             mask_blocks.append(mask_b)
             if b == 0:
                 wc = held.tile([P, C_BLOCKS, R + 1], F32, name="wc")
                 wn = held.tile([P, C_BLOCKS, R + 1], F32, name="wn")
                 wp = held.tile([P, C_BLOCKS, 1], F32, name="wp")
-                nc.sync.dma_start(wn[:], w_n.rearrange("(b c) k -> c b k", c=P))
-                nc.sync.dma_start(wc[:], w_c.rearrange("(b c) k -> c b k", c=P))
-                nc.sync.dma_start(wp[:], w_p.rearrange("(b c) k -> c b k", c=P))
+                nc.sync.dma_start(wn[:], w_n.rearrange("(q b) k -> q b k", b=C_BLOCKS))
+                nc.sync.dma_start(wc[:], w_c.rearrange("(q b) k -> q b k", b=C_BLOCKS))
+                nc.sync.dma_start(wp[:], w_p.rearrange("(q b) k -> q b k", b=C_BLOCKS))
         for b in range(C_BLOCKS):
-            nc.sync.dma_start(mask_blocks[b][:, S:N], nbr_w[b * P : (b + 1) * P, S:N])
+            nc.sync.dma_start(mask_blocks[b][:, S:N], mask_view[:, b, S:N])
         p_f32 = held.tile([P, C_BLOCKS, PHRASES], F32, name="p_f32")
-        nc.sync.dma_start(p_f32[:], p.rearrange("(b c) i -> c b i", c=P))
+        nc.sync.dma_start(p_f32[:], p.rearrange("(q b) i -> q b i", b=C_BLOCKS))
 
         ones_f32 = held.tile([P, P], F32, name="ones_f32")
         nc.gpsimd.memset(ones_f32[:], 1.0)
         ones = held.tile([P, P], BF16, name="ones")
         nc.scalar.copy(ones[:], ones_f32[:])
-        cross = []
-        nodew = []
-        for b in range(C_BLOCKS):
-            cross_b = held.tile([P, S], F32, name=f"cross{b}_0")
-            nodew_b = held.tile([P, S], F32, name=f"nodew{b}_0")
-            nc.scalar.activation(cross_b[:], x_blocks[b][:], IDENTITY, bias=wp[:, b, :], scale=wc[:, b, 0:1])
-            nc.scalar.activation(nodew_b[:], x_blocks[b][:], COPY, scale=wn[:, b, 0:1])
-            cross.append(cross_b)
-            nodew.append(nodew_b)
+        identity = held.tile([P, P], F32, name="identity")
+        make_identity(nc, identity[:])
 
+        nodew = []
+        cross_sums = []
+        for b in range(C_BLOCKS):
+            nodew_b = held.tile([P, S], F32, name=f"nodew{b}_0")
+            nc.scalar.activation(nodew_b[:], x_blocks[b][:], COPY, scale=wn[:, b, 0:1])
+            nodew.append(nodew_b)
+            cross_sum = psum.tile([P, S], F32, name=f"cross_sum{b}")
+            product = held.tile([P, S], F32, name=f"product{b}_0")
+            nc.scalar.activation(product[:], x_blocks[b][:], IDENTITY, bias=wp[:, b, :], scale=wc[:, b, 0:1])
+            nc.tensor.matmul(cross_sum[:], identity[:], product[:], start=True, stop=False)
+            cross_sums.append(cross_sum)
+
+        last_t = []
         for r in range(1, R + 1):
             for b in range(C_BLOCKS):
                 t = held.tile([P, S], F32, name=f"t{b}_{r}")
                 neighbour = offsets[:, (r - 1) * OFFSET_COLUMNS : r * OFFSET_COLUMNS]
                 nc.vector.tensor_tensor(t[:], x_blocks[b][:].indirect(neighbour), mask_blocks[b][:, (r - 1) * S : r * S], MULT)
 
-                sum_dt = BF16 if r == R else F32
-                cross_next = held.tile([P, S], sum_dt, name=f"cross{b}_{r}")
-                nodew_next = held.tile([P, S], sum_dt, name=f"nodew{b}_{r}")
-                nc.vector.scalar_tensor_tensor(cross_next[:], t[:], wc[:, b, r : r + 1], cross[b][:], MULT, ADD)
+                nodew_next = held.tile([P, S], BF16 if r == R else F32, name=f"nodew{b}_{r}")
                 nc.vector.scalar_tensor_tensor(nodew_next[:], t[:], wn[:, b, r : r + 1], nodew[b][:], MULT, ADD)
-                cross[b] = cross_next
                 nodew[b] = nodew_next
+                if r < R:
+                    product = held.tile([P, S], F32, name=f"product{b}_{r}")
+                    nc.scalar.activation(product[:], t[:], COPY, scale=wc[:, b, r : r + 1])
+                    nc.tensor.matmul(cross_sums[b][:], identity[:], product[:], start=False, stop=(r == R - 1))
+                else:
+                    last_t.append(t)
 
         scores = [psum.tile([P, S], F32, name=f"scores{i}") for i in range(PHRASE_BLOCKS)]
         for b in range(C_BLOCKS):
+            for i in range(PHRASE_BLOCKS):
+                nc.tensor.matmul(scores[i][:], ones[:], nodew[b][:], start=(b == 0), stop=False)
+        for b in range(C_BLOCKS):
             p_bf = held.tile([P, PHRASES], BF16, name=f"p_bf{b}")
             nc.scalar.copy(p_bf[:], p_f32[:, b, :])
+            cross = held.tile([P, S], BF16, name=f"cross{b}")
+            nc.vector.scalar_tensor_tensor(cross[:], last_t[b][:], wc[:, b, R : R + 1], cross_sums[b][:], MULT, ADD)
             for i in range(PHRASE_BLOCKS):
-                nc.tensor.matmul(scores[i][:], p_bf[:, i * P : (i + 1) * P], cross[b][:], start=(b == 0), stop=False)
-            for i in range(PHRASE_BLOCKS):
-                nc.tensor.matmul(scores[i][:], ones[:], nodew[b][:], start=False, stop=(b == C_BLOCKS - 1))
+                nc.tensor.matmul(
+                    scores[i][:], p_bf[:, i * P : (i + 1) * P], cross[:], start=False, stop=(b == C_BLOCKS - 1)
+                )
 
         for i in range(PHRASE_BLOCKS):
             result = held.tile([P, S], F32, name=f"result{i}")

@@ -29,30 +29,28 @@ def tile_encodingmodel_kernel(tc, x, p, w_p, w_n, w_c, nbr_w, offs, out):
         tc.tile_pool(name="held", bufs=1) as held,
         tc.psum_pool(name="psum", bufs=1) as psum,
     ):
-        offsets = held.tile([P, N // 16], U16, name="offsets")
-        nc.sync.dma_start(offsets[:], offs)
-
         x_view = x.rearrange("(q b) s -> q b s", b=C_BLOCKS)
-        mask_view = nbr_w.rearrange("(q b) j -> q b j", b=C_BLOCKS)
-        x_blocks = []
-        mask_blocks = []
-        for b in range(C_BLOCKS):
-            x_b = held.tile([P, S], F32, name=f"x{b}")
-            nc.sync.dma_start(x_b[:], x_view[:, b, :])
-            x_blocks.append(x_b)
-            mask_b = held.tile([P, N], F32, name=f"mask{b}")
-            nc.sync.dma_start(mask_b[:, 0:S], mask_view[:, b, 0:S])
-            mask_blocks.append(mask_b)
-            if b == 0:
-                wc = held.tile([P, C_BLOCKS, R + 1], F32, name="wc")
-                wn = held.tile([P, C_BLOCKS, R + 1], F32, name="wn")
-                wp = held.tile([P, C_BLOCKS, 1], F32, name="wp")
-                nc.sync.dma_start(wn[:], w_n.rearrange("(q b) k -> q b k", b=C_BLOCKS))
-                nc.sync.dma_start(wc[:], w_c.rearrange("(q b) k -> q b k", b=C_BLOCKS))
-                nc.sync.dma_start(wp[:], w_p.rearrange("(q b) k -> q b k", b=C_BLOCKS))
-        for b in range(C_BLOCKS):
-            nc.sync.dma_start(mask_blocks[b][:, S:N], mask_view[:, b, S:N])
+        offsets = held.tile([P, N // 16], U16, name="offsets")
+        x_blocks = [held.tile([P, S], F32, name=f"x{b}") for b in range(C_BLOCKS)]
+        nbr_mask = held.tile([P, N], F32, name="nbr_mask")
+        wc = held.tile([P, C_BLOCKS, R + 1], F32, name="wc")
+        wn = held.tile([P, C_BLOCKS, R + 1], F32, name="wn")
+        wp = held.tile([P, C_BLOCKS, 1], F32, name="wp")
         p_f32 = held.tile([P, C_BLOCKS, PHRASES], F32, name="p_f32")
+
+        def load_mask(r):
+            nc.sync.dma_start(nbr_mask[:, (r - 1) * S : r * S], nbr_w[0:P, (r - 1) * S : r * S])
+
+        nc.sync.dma_start(offsets[:], offs)
+        nc.sync.dma_start(x_blocks[0][:], x_view[:, 0, :])
+        load_mask(1)
+        nc.sync.dma_start(wc[:], w_c.rearrange("(q b) k -> q b k", b=C_BLOCKS))
+        nc.sync.dma_start(x_blocks[1][:], x_view[:, 1, :])
+        load_mask(2)
+        nc.sync.dma_start(wn[:], w_n.rearrange("(q b) k -> q b k", b=C_BLOCKS))
+        load_mask(3)
+        nc.sync.dma_start(wp[:], w_p.rearrange("(q b) k -> q b k", b=C_BLOCKS))
+        load_mask(4)
         nc.sync.dma_start(p_f32[:], p.rearrange("(q b) i -> q b i", b=C_BLOCKS))
 
         ones_f32 = held.tile([P, P], F32, name="ones_f32")
@@ -62,34 +60,46 @@ def tile_encodingmodel_kernel(tc, x, p, w_p, w_n, w_c, nbr_w, offs, out):
         identity = held.tile([P, P], F32, name="identity")
         make_identity(nc, identity[:])
 
-        nodew = []
-        cross_sums = []
-        for b in range(C_BLOCKS):
-            nodew_b = held.tile([P, S], F32, name=f"nodew{b}_0")
-            nc.scalar.activation(nodew_b[:], x_blocks[b][:], COPY, scale=wn[:, b, 0:1])
-            nodew.append(nodew_b)
-            cross_sum = psum.tile([P, S], F32, name=f"cross_sum{b}")
-            product = held.tile([P, S], F32, name=f"product{b}_0")
-            nc.scalar.activation(product[:], x_blocks[b][:], IDENTITY, bias=wp[:, b, :], scale=wc[:, b, 0:1])
-            nc.tensor.matmul(cross_sum[:], identity[:], product[:], start=True, stop=False)
-            cross_sums.append(cross_sum)
+        cross_sums = [psum.tile([P, S], F32, name=f"cross_sum{b}") for b in range(C_BLOCKS)]
+        t = {}
+        nodew = {}
 
-        last_t = []
+        def look_up(b, r):
+            t[b, r] = held.tile([P, S], F32, name=f"t{b}_{r}")
+            neighbour = offsets[:, (r - 1) * OFFSET_COLUMNS : r * OFFSET_COLUMNS]
+            nc.vector.tensor_tensor(t[b, r][:], x_blocks[b][:].indirect(neighbour), nbr_mask[:, (r - 1) * S : r * S], MULT)
+
+        def add_to_cross(b, r):
+            product = held.tile([P, S], F32, name=f"product{b}_{r}")
+            feature = x_blocks[b] if r == 0 else t[b, r]
+            if r == R - 1:
+                nc.scalar.activation(product[:], feature[:], IDENTITY, bias=wp[:, b, :], scale=wc[:, b, r : r + 1])
+            else:
+                nc.scalar.activation(product[:], feature[:], COPY, scale=wc[:, b, r : r + 1])
+            nc.tensor.matmul(cross_sums[b][:], identity[:], product[:], start=(r == 0), stop=(r == R - 1))
+
+        def add_to_nodew(b, r):
+            nodew_next = held.tile([P, S], BF16 if r == R else F32, name=f"nodew{b}_{r}")
+            nc.vector.scalar_tensor_tensor(nodew_next[:], t[b, r][:], wn[:, b, r : r + 1], nodew[b][:], MULT, ADD)
+            nodew[b] = nodew_next
+
+        for b in range(C_BLOCKS):
+            add_to_cross(b, 0)
         for r in range(1, R + 1):
             for b in range(C_BLOCKS):
-                t = held.tile([P, S], F32, name=f"t{b}_{r}")
-                neighbour = offsets[:, (r - 1) * OFFSET_COLUMNS : r * OFFSET_COLUMNS]
-                nc.vector.tensor_tensor(t[:], x_blocks[b][:].indirect(neighbour), mask_blocks[b][:, (r - 1) * S : r * S], MULT)
-
-                nodew_next = held.tile([P, S], BF16 if r == R else F32, name=f"nodew{b}_{r}")
-                nc.vector.scalar_tensor_tensor(nodew_next[:], t[:], wn[:, b, r : r + 1], nodew[b][:], MULT, ADD)
-                nodew[b] = nodew_next
-                if r < R:
-                    product = held.tile([P, S], F32, name=f"product{b}_{r}")
-                    nc.scalar.activation(product[:], t[:], COPY, scale=wc[:, b, r : r + 1])
-                    nc.tensor.matmul(cross_sums[b][:], identity[:], product[:], start=False, stop=(r == R - 1))
-                else:
-                    last_t.append(t)
+                look_up(b, r)
+            if r == 2:
+                for b in range(C_BLOCKS):
+                    nodew[b] = held.tile([P, S], F32, name=f"nodew{b}_0")
+                    nc.scalar.activation(nodew[b][:], x_blocks[b][:], COPY, scale=wn[:, b, 0:1])
+            if r < R:
+                for b in range(C_BLOCKS):
+                    add_to_cross(b, r)
+            if r > 1:
+                for b in range(C_BLOCKS):
+                    add_to_nodew(b, r - 1)
+        for b in range(C_BLOCKS):
+            add_to_nodew(b, R)
 
         scores = [psum.tile([P, S], F32, name=f"scores{i}") for i in range(PHRASE_BLOCKS)]
         for b in range(C_BLOCKS):
@@ -99,7 +109,7 @@ def tile_encodingmodel_kernel(tc, x, p, w_p, w_n, w_c, nbr_w, offs, out):
             p_bf = held.tile([P, PHRASES], BF16, name=f"p_bf{b}")
             nc.scalar.copy(p_bf[:], p_f32[:, b, :])
             cross = held.tile([P, S], BF16, name=f"cross{b}")
-            nc.vector.scalar_tensor_tensor(cross[:], last_t[b][:], wc[:, b, R : R + 1], cross_sums[b][:], MULT, ADD)
+            nc.vector.scalar_tensor_tensor(cross[:], t[b, R][:], wc[:, b, R : R + 1], cross_sums[b][:], MULT, ADD)
             for i in range(PHRASE_BLOCKS):
                 nc.tensor.matmul(
                     scores[i][:], p_bf[:, i * P : (i + 1) * P], cross[:], start=False, stop=(b == C_BLOCKS - 1)

@@ -115,11 +115,7 @@ def tile_encodingmodel_kernel(tc, x, p, w_p, w_n, w_c, nbr_w, offs, out):
                     scores[i][:], p_bf[:, i * P : (i + 1) * P], cross[:], start=False, stop=(b == C_BLOCKS - 1)
                 )
 
-        for i in range(PHRASE_BLOCKS):
-            result = held.tile([P, S], F32, name=f"result{i}")
-            if i % 2 == 0:
-                nc.vector.tensor_scalar_add(result[:], scores[i][:], SCORE_B)
-                nc.sync.dma_start(out[i * P : (i + 1) * P, :], result[:])
-            else:
-                nc.scalar.activation(result[:], scores[i][:], COPY, bias=SCORE_B)
-                nc.scalar.dma_start(out[i * P : (i + 1) * P, :], result[:])
+        result = held.tile([P, PHRASE_BLOCKS, S], F32, name="result")
+        nc.vector.tensor_scalar_add(result[:, 0, :], scores[0][:], SCORE_B)
+        nc.scalar.activation(result[:, 1, :], scores[1][:], COPY, bias=SCORE_B)
+        nc.sync.dma_start(out.rearrange("(i q) s -> q i s", i=PHRASE_BLOCKS), result[:])

@@ -108,14 +108,15 @@ def tile_encodingmodel_kernel(tc, x, p, w_p, w_n, w_c, nbr_w, offs, out):
         for b in range(C_BLOCKS):
             p_bf = held.tile([P, PHRASES], BF16, name=f"p_bf{b}")
             nc.scalar.copy(p_bf[:], p_f32[:, b, :])
+            p_pairs = p_bf[:].rearrange("q (m i) -> q i m", i=PHRASE_BLOCKS)
             cross = held.tile([P, S], BF16, name=f"cross{b}")
             nc.vector.scalar_tensor_tensor(cross[:], t[b, R][:], wc[:, b, R : R + 1], cross_sums[b][:], MULT, ADD)
             for i in range(PHRASE_BLOCKS):
                 nc.tensor.matmul(
-                    scores[i][:], p_bf[:, i * P : (i + 1) * P], cross[:], start=False, stop=(b == C_BLOCKS - 1)
+                    scores[i][:], p_pairs[:, i, :], cross[:], start=False, stop=(b == C_BLOCKS - 1)
                 )
 
         result = held.tile([P, PHRASE_BLOCKS, S], F32, name="result")
         nc.vector.tensor_scalar_add(result[:, 0, :], scores[0][:], SCORE_B)
         nc.scalar.activation(result[:, 1, :], scores[1][:], COPY, bias=SCORE_B)
-        nc.sync.dma_start(out.rearrange("(i q) s -> q i s", i=PHRASE_BLOCKS), result[:])
+        nc.sync.dma_start(out.rearrange("(q i) s -> q i s", i=PHRASE_BLOCKS), result[:])

@@ -38,29 +38,32 @@ def tile_encodingmodel_kernel(tc, x, p, w_p, w_n, w_c, nbr_w, offs, out):
         wp = held.tile([P, C_BLOCKS, 1], F32, name="wp")
         p_f32 = held.tile([P, C_BLOCKS, PHRASES], F32, name="p_f32")
 
-        def load_mask(r):
-            nc.sync.dma_start(nbr_mask[:, (r - 1) * S : r * S], nbr_w[0:P, (r - 1) * S : r * S])
+        def load_masks(first, last):
+            columns = slice((first - 1) * S, last * S)
+            nc.sync.dma_start(nbr_mask[:, columns], nbr_w[0:P, columns])
 
         nc.sync.dma_start(offsets[:], offs)
         nc.sync.dma_start(x_blocks[0][:], x_view[:, 0, :])
-        load_mask(1)
+        load_masks(1, 1)
         nc.sync.dma_start(wc[:], w_c.rearrange("(q b) k -> q b k", b=C_BLOCKS))
         nc.sync.dma_start(x_blocks[1][:], x_view[:, 1, :])
-        load_mask(2)
+        load_masks(2, 2)
+        load_masks(3, 4)
         nc.sync.dma_start(wn[:], w_n.rearrange("(q b) k -> q b k", b=C_BLOCKS))
-        load_mask(3)
         nc.sync.dma_start(wp[:], w_p.rearrange("(q b) k -> q b k", b=C_BLOCKS))
-        load_mask(4)
         nc.sync.dma_start(p_f32[:], p.rearrange("(q b) i -> q b i", b=C_BLOCKS))
 
         ones_f32 = held.tile([P, P], F32, name="ones_f32")
         nc.gpsimd.memset(ones_f32[:], 1.0)
+        constant_share = held.tile([P, S], F32, name="constant_share")
+        nc.vector.memset(constant_share[:], SCORE_B / P)
         ones = held.tile([P, P], BF16, name="ones")
         nc.scalar.copy(ones[:], ones_f32[:])
         identity = held.tile([P, P], F32, name="identity")
         make_identity(nc, identity[:])
 
         cross_sums = [psum.tile([P, S], F32, name=f"cross_sum{b}") for b in range(C_BLOCKS)]
+        last_term_in_psum = [R, R - 1]
         t = {}
         nodew = {}
 
@@ -72,11 +75,11 @@ def tile_encodingmodel_kernel(tc, x, p, w_p, w_n, w_c, nbr_w, offs, out):
         def add_to_cross(b, r):
             product = held.tile([P, S], F32, name=f"product{b}_{r}")
             feature = x_blocks[b] if r == 0 else t[b, r]
-            if r == R - 1:
+            if r == last_term_in_psum[b]:
                 nc.scalar.activation(product[:], feature[:], IDENTITY, bias=wp[:, b, :], scale=wc[:, b, r : r + 1])
             else:
                 nc.scalar.activation(product[:], feature[:], COPY, scale=wc[:, b, r : r + 1])
-            nc.tensor.matmul(cross_sums[b][:], identity[:], product[:], start=(r == 0), stop=(r == R - 1))
+            nc.tensor.matmul(cross_sums[b][:], identity[:], product[:], start=(r == 0), stop=(r == last_term_in_psum[b]))
 
         def add_to_nodew(b, r):
             nodew_next = held.tile([P, S], BF16 if r == R else F32, name=f"nodew{b}_{r}")
@@ -85,38 +88,49 @@ def tile_encodingmodel_kernel(tc, x, p, w_p, w_n, w_c, nbr_w, offs, out):
 
         for b in range(C_BLOCKS):
             add_to_cross(b, 0)
-        for r in range(1, R + 1):
+        for b in range(C_BLOCKS):
+            nodew[b] = held.tile([P, S], F32, name=f"nodew{b}_0")
+            nc.scalar.activation(nodew[b][:], x_blocks[b][:], COPY, scale=wn[:, b, 0:1])
+        for r in (1, 2):
             for b in range(C_BLOCKS):
                 look_up(b, r)
-            if r == 2:
-                for b in range(C_BLOCKS):
-                    nodew[b] = held.tile([P, S], F32, name=f"nodew{b}_0")
-                    nc.scalar.activation(nodew[b][:], x_blocks[b][:], COPY, scale=wn[:, b, 0:1])
-            if r < R:
-                for b in range(C_BLOCKS):
-                    add_to_cross(b, r)
-            if r > 1:
-                for b in range(C_BLOCKS):
-                    add_to_nodew(b, r - 1)
-        for b in range(C_BLOCKS):
-            add_to_nodew(b, R)
+                add_to_cross(b, r)
+        look_up(0, 3)
+        add_to_cross(0, 3)
+        add_to_nodew(0, 1)
+        look_up(0, 4)
+        add_to_cross(0, 4)
+        add_to_nodew(0, 2)
+        look_up(1, 3)
+        add_to_cross(1, 3)
+        add_to_nodew(1, 1)
+        add_to_nodew(0, 3)
+        look_up(1, 4)
+        add_to_nodew(1, 2)
+        add_to_nodew(0, 4)
+        add_to_nodew(1, 3)
 
         scores = [psum.tile([P, S], F32, name=f"scores{i}") for i in range(PHRASE_BLOCKS)]
-        for b in range(C_BLOCKS):
-            for i in range(PHRASE_BLOCKS):
-                nc.tensor.matmul(scores[i][:], ones[:], nodew[b][:], start=(b == 0), stop=False)
+        for i in range(PHRASE_BLOCKS):
+            nc.tensor.matmul(scores[i][:], ones_f32[:], constant_share[:], start=True, stop=False)
+        p_pairs = []
         for b in range(C_BLOCKS):
             p_bf = held.tile([P, PHRASES], BF16, name=f"p_bf{b}")
             nc.scalar.copy(p_bf[:], p_f32[:, b, :])
-            p_pairs = p_bf[:].rearrange("q (m i) -> q i m", i=PHRASE_BLOCKS)
-            cross = held.tile([P, S], BF16, name=f"cross{b}")
-            nc.vector.scalar_tensor_tensor(cross[:], t[b, R][:], wc[:, b, R : R + 1], cross_sums[b][:], MULT, ADD)
+            p_pairs.append(p_bf[:].rearrange("q (m i) -> q i m", i=PHRASE_BLOCKS))
+        cross = [held.tile([P, S], BF16, name=f"cross{b}") for b in range(C_BLOCKS)]
+        nc.scalar.copy(cross[0][:], cross_sums[0][:])
+        add_to_nodew(1, 4)
+        nc.vector.scalar_tensor_tensor(cross[1][:], t[1, R][:], wc[:, 1, R : R + 1], cross_sums[1][:], MULT, ADD)
+        for i in range(PHRASE_BLOCKS):
+            nc.tensor.matmul(scores[i][:], p_pairs[0][:, i, :], cross[0][:], start=False, stop=False)
+        for b in range(C_BLOCKS):
             for i in range(PHRASE_BLOCKS):
-                nc.tensor.matmul(
-                    scores[i][:], p_pairs[:, i, :], cross[:], start=False, stop=(b == C_BLOCKS - 1)
-                )
+                nc.tensor.matmul(scores[i][:], ones[:], nodew[b][:], start=False, stop=False)
+        for i in range(PHRASE_BLOCKS):
+            nc.tensor.matmul(scores[i][:], p_pairs[1][:, i, :], cross[1][:], start=False, stop=True)
 
         result = held.tile([P, PHRASE_BLOCKS, S], F32, name="result")
-        nc.vector.tensor_scalar_add(result[:, 0, :], scores[0][:], SCORE_B)
-        nc.scalar.activation(result[:, 1, :], scores[1][:], COPY, bias=SCORE_B)
+        nc.vector.tensor_copy(result[:, 0, :], scores[0][:])
+        nc.scalar.copy(result[:, 1, :], scores[1][:])
         nc.sync.dma_start(out.rearrange("(q i) s -> q i s", i=PHRASE_BLOCKS), result[:])

@@ -55,7 +55,7 @@ def tile_encodingmodel_kernel(tc, x, p, w_p, w_n, w_c, nbr_w, offs, out):
 
         ones_f32 = held.tile([P, P], F32, name="ones_f32")
         nc.gpsimd.memset(ones_f32[:], 1.0)
-        constant_share = held.tile([P, S], F32, name="constant_share")
+        constant_share = held.tile([P, P], F32, name="constant_share")
         nc.vector.memset(constant_share[:], SCORE_B / P)
         ones = held.tile([P, P], BF16, name="ones")
         nc.scalar.copy(ones[:], ones_f32[:])
@@ -86,15 +86,18 @@ def tile_encodingmodel_kernel(tc, x, p, w_p, w_n, w_c, nbr_w, offs, out):
             nc.vector.scalar_tensor_tensor(nodew_next[:], t[b, r][:], wn[:, b, r : r + 1], nodew[b][:], MULT, ADD)
             nodew[b] = nodew_next
 
-        for b in range(C_BLOCKS):
-            add_to_cross(b, 0)
+        add_to_cross(0, 0)
         for b in range(C_BLOCKS):
             nodew[b] = held.tile([P, S], F32, name=f"nodew{b}_0")
             nc.scalar.activation(nodew[b][:], x_blocks[b][:], COPY, scale=wn[:, b, 0:1])
-        for r in (1, 2):
-            for b in range(C_BLOCKS):
-                look_up(b, r)
-                add_to_cross(b, r)
+        look_up(0, 1)
+        add_to_cross(0, 1)
+        add_to_cross(1, 0)
+        look_up(1, 1)
+        add_to_cross(1, 1)
+        for b in range(C_BLOCKS):
+            look_up(b, 2)
+            add_to_cross(b, 2)
         look_up(0, 3)
         add_to_cross(0, 3)
         add_to_nodew(0, 1)
@@ -110,9 +113,12 @@ def tile_encodingmodel_kernel(tc, x, p, w_p, w_n, w_c, nbr_w, offs, out):
         add_to_nodew(0, 4)
         add_to_nodew(1, 3)
 
-        scores = [psum.tile([P, S], F32, name=f"scores{i}") for i in range(PHRASE_BLOCKS)]
-        for i in range(PHRASE_BLOCKS):
-            nc.tensor.matmul(scores[i][:], ones_f32[:], constant_share[:], start=True, stop=False)
+        halves = [slice(h * P, (h + 1) * P) for h in range(S // P)]
+        scores = {
+            (i, h): psum.tile([P, P], F32, name=f"scores{i}_{h}") for h in range(S // P) for i in range(PHRASE_BLOCKS)
+        }
+        for tile in scores.values():
+            nc.tensor.matmul(tile[:], ones_f32[:], constant_share[:], start=True, stop=False)
         p_pairs = []
         for b in range(C_BLOCKS):
             p_bf = held.tile([P, PHRASES], BF16, name=f"p_bf{b}")
@@ -121,16 +127,25 @@ def tile_encodingmodel_kernel(tc, x, p, w_p, w_n, w_c, nbr_w, offs, out):
         cross = [held.tile([P, S], BF16, name=f"cross{b}") for b in range(C_BLOCKS)]
         nc.scalar.copy(cross[0][:], cross_sums[0][:])
         add_to_nodew(1, 4)
-        nc.vector.scalar_tensor_tensor(cross[1][:], t[1, R][:], wc[:, 1, R : R + 1], cross_sums[1][:], MULT, ADD)
-        for i in range(PHRASE_BLOCKS):
-            nc.tensor.matmul(scores[i][:], p_pairs[0][:, i, :], cross[0][:], start=False, stop=False)
-        for b in range(C_BLOCKS):
-            for i in range(PHRASE_BLOCKS):
-                nc.tensor.matmul(scores[i][:], ones[:], nodew[b][:], start=False, stop=False)
-        for i in range(PHRASE_BLOCKS):
-            nc.tensor.matmul(scores[i][:], p_pairs[1][:, i, :], cross[1][:], start=False, stop=True)
+        for half in halves:
+            nc.vector.scalar_tensor_tensor(
+                cross[1][:, half], t[1, R][:, half], wc[:, 1, R : R + 1], cross_sums[1][:, half], MULT, ADD
+            )
 
+        def add_to_scores(h, feature, weights, stop=False):
+            for i in range(PHRASE_BLOCKS):
+                nc.tensor.matmul(scores[i, h][:], weights[i], feature[:, halves[h]], start=False, stop=stop)
+
+        all_ones = [ones[:]] * PHRASE_BLOCKS
+        p_weights = [[pairs[:, i, :] for i in range(PHRASE_BLOCKS)] for pairs in p_pairs]
         result = held.tile([P, PHRASE_BLOCKS, S], F32, name="result")
-        nc.vector.tensor_copy(result[:, 0, :], scores[0][:])
-        nc.scalar.copy(result[:, 1, :], scores[1][:])
+        for h in range(S // P):
+            add_to_scores(h, cross[0], p_weights[0])
+        for h in range(S // P):
+            add_to_scores(h, nodew[0], all_ones)
+        for h in range(S // P):
+            add_to_scores(h, nodew[1], all_ones)
+            add_to_scores(h, cross[1], p_weights[1], stop=True)
+            nc.vector.tensor_copy(result[:, 0, halves[h]], scores[0, h][:])
+            nc.scalar.copy(result[:, 1, halves[h]], scores[1, h][:])
         nc.sync.dma_start(out.rearrange("(q i) s -> q i s", i=PHRASE_BLOCKS), result[:])

@@ -55,7 +55,7 @@ def tile_encodingmodel_kernel(tc, x, p, w_p, w_n, w_c, nbr_w, offs, out):
 
         ones_f32 = held.tile([P, P], F32, name="ones_f32")
         nc.gpsimd.memset(ones_f32[:], 1.0)
-        constant_share = held.tile([P, P], F32, name="constant_share")
+        constant_share = held.tile([P, S], F32, name="constant_share")
         nc.vector.memset(constant_share[:], SCORE_B / P)
         ones = held.tile([P, P], BF16, name="ones")
         nc.scalar.copy(ones[:], ones_f32[:])
@@ -113,12 +113,12 @@ def tile_encodingmodel_kernel(tc, x, p, w_p, w_n, w_c, nbr_w, offs, out):
         add_to_nodew(0, 4)
         add_to_nodew(1, 3)
 
-        halves = [slice(h * P, (h + 1) * P) for h in range(S // P)]
+        parts = [slice(0, 3 * S // 4), slice(3 * S // 4, S)]
         scores = {
-            (i, h): psum.tile([P, P], F32, name=f"scores{i}_{h}") for h in range(S // P) for i in range(PHRASE_BLOCKS)
+            (i, h): psum.tile([P, parts[h].stop - parts[h].start], F32, name=f"scores{i}_{h}") for h in range(len(parts)) for i in range(PHRASE_BLOCKS)
         }
-        for tile in scores.values():
-            nc.tensor.matmul(tile[:], ones_f32[:], constant_share[:], start=True, stop=False)
+        for (i, h), tile in scores.items():
+            nc.tensor.matmul(tile[:], ones_f32[:], constant_share[:, parts[h]], start=True, stop=False)
         p_pairs = []
         for b in range(C_BLOCKS):
             p_bf = held.tile([P, PHRASES], BF16, name=f"p_bf{b}")
@@ -127,25 +127,25 @@ def tile_encodingmodel_kernel(tc, x, p, w_p, w_n, w_c, nbr_w, offs, out):
         cross = [held.tile([P, S], BF16, name=f"cross{b}") for b in range(C_BLOCKS)]
         nc.scalar.copy(cross[0][:], cross_sums[0][:])
         add_to_nodew(1, 4)
-        for half in halves:
+        for part in parts:
             nc.vector.scalar_tensor_tensor(
-                cross[1][:, half], t[1, R][:, half], wc[:, 1, R : R + 1], cross_sums[1][:, half], MULT, ADD
+                cross[1][:, part], t[1, R][:, part], wc[:, 1, R : R + 1], cross_sums[1][:, part], MULT, ADD
             )
 
         def add_to_scores(h, feature, weights, stop=False):
             for i in range(PHRASE_BLOCKS):
-                nc.tensor.matmul(scores[i, h][:], weights[i], feature[:, halves[h]], start=False, stop=stop)
+                nc.tensor.matmul(scores[i, h][:], weights[i], feature[:, parts[h]], start=False, stop=stop)
 
         all_ones = [ones[:]] * PHRASE_BLOCKS
         p_weights = [[pairs[:, i, :] for i in range(PHRASE_BLOCKS)] for pairs in p_pairs]
         result = held.tile([P, PHRASE_BLOCKS, S], F32, name="result")
-        for h in range(S // P):
+        for h in range(len(parts)):
             add_to_scores(h, cross[0], p_weights[0])
-        for h in range(S // P):
+        for h in range(len(parts)):
             add_to_scores(h, nodew[0], all_ones)
-        for h in range(S // P):
+        for h in range(len(parts)):
             add_to_scores(h, nodew[1], all_ones)
             add_to_scores(h, cross[1], p_weights[1], stop=True)
-            nc.vector.tensor_copy(result[:, 0, halves[h]], scores[0, h][:])
-            nc.scalar.copy(result[:, 1, halves[h]], scores[1, h][:])
+            nc.vector.tensor_copy(result[:, 0, parts[h]], scores[0, h][:])
+            nc.scalar.copy(result[:, 1, parts[h]], scores[1, h][:])
         nc.sync.dma_start(out.rearrange("(q i) s -> q i s", i=PHRASE_BLOCKS), result[:])

@@ -45,8 +45,8 @@ def tile_encodingmodel_kernel(tc, x, p, w_p, w_n, w_c, nbr_w, offs, out):
         nc.sync.dma_start(offsets[:], offs)
         nc.sync.dma_start(x_blocks[0][:], x_view[:, 0, :])
         load_masks(1, 1)
-        nc.sync.dma_start(wc[:], w_c.rearrange("(q b) k -> q b k", b=C_BLOCKS))
         nc.sync.dma_start(x_blocks[1][:], x_view[:, 1, :])
+        nc.sync.dma_start(wc[:], w_c.rearrange("(q b) k -> q b k", b=C_BLOCKS))
         load_masks(2, 2)
         load_masks(3, 4)
         nc.sync.dma_start(wn[:], w_n.rearrange("(q b) k -> q b k", b=C_BLOCKS))

import concourse.mybir as mybir
from concourse.masks import make_identity

F32 = mybir.dt.float32
BF16 = mybir.dt.bfloat16
U16 = mybir.dt.uint16
MULT = mybir.AluOpType.mult
ADD = mybir.AluOpType.add
IDENTITY = mybir.ActivationFunctionType.Identity
COPY = mybir.ActivationFunctionType.Copy

P = 128
C = 256
S = 256
PHRASES = 256
R = 4
N = R * S
C_BLOCKS = C // P
PHRASE_BLOCKS = PHRASES // P
OFFSET_COLUMNS = S // 16
SCORE_B = 0.25

FLOPS = 2 * C * S * (PHRASES + 1)


def tile_encodingmodel_kernel(tc, x, p, w_p, w_n, w_c, nbr_w, offs, out):
    nc = tc.nc
    with (
        tc.tile_pool(name="held", bufs=1) as held,
        tc.psum_pool(name="psum", bufs=1) as psum,
    ):
        x_view = x.rearrange("(q b) s -> q b s", b=C_BLOCKS)
        offsets = held.tile([P, N // 16], U16, name="offsets")
        x_blocks = [held.tile([P, S], F32, name=f"x{b}") for b in range(C_BLOCKS)]
        nbr_mask = held.tile([P, N], F32, name="nbr_mask")
        wc = held.tile([P, C_BLOCKS, R + 1], F32, name="wc")
        wn = held.tile([P, C_BLOCKS, R + 1], F32, name="wn")
        wp = held.tile([P, C_BLOCKS, 1], F32, name="wp")
        p_f32 = held.tile([P, C_BLOCKS, PHRASES], F32, name="p_f32")

        def load_masks(first, last):
            columns = slice((first - 1) * S, last * S)
            nc.sync.dma_start(nbr_mask[:, columns], nbr_w[0:P, columns])

        nc.sync.dma_start(offsets[:], offs)
        nc.sync.dma_start(x_blocks[0][:], x_view[:, 0, :])
        load_masks(1, 1)
        nc.sync.dma_start(x_blocks[1][:], x_view[:, 1, :])
        nc.sync.dma_start(wc[:], w_c.rearrange("(q b) k -> q b k", b=C_BLOCKS))
        load_masks(2, 2)
        load_masks(3, 4)
        nc.sync.dma_start(wn[:], w_n.rearrange("(q b) k -> q b k", b=C_BLOCKS))
        nc.sync.dma_start(wp[:], w_p.rearrange("(q b) k -> q b k", b=C_BLOCKS))
        nc.sync.dma_start(p_f32[:], p.rearrange("(q b) i -> q b i", b=C_BLOCKS))

        ones_f32 = held.tile([P, P], F32, name="ones_f32")
        nc.gpsimd.memset(ones_f32[:], 1.0)
        constant_share = held.tile([P, S], F32, name="constant_share")
        nc.vector.memset(constant_share[:], SCORE_B / P)
        ones = held.tile([P, P], BF16, name="ones")
        nc.scalar.copy(ones[:], ones_f32[:])
        identity = held.tile([P, P], F32, name="identity")
        make_identity(nc, identity[:])

        cross_sums = [psum.tile([P, S], F32, name=f"cross_sum{b}") for b in range(C_BLOCKS)]
        last_term_in_psum = [R, R - 1]
        t = {}
        nodew = {}

        def look_up(b, r):
            t[b, r] = held.tile([P, S], F32, name=f"t{b}_{r}")
            neighbour = offsets[:, (r - 1) * OFFSET_COLUMNS : r * OFFSET_COLUMNS]
            nc.vector.tensor_tensor(t[b, r][:], x_blocks[b][:].indirect(neighbour), nbr_mask[:, (r - 1) * S : r * S], MULT)

        def add_to_cross(b, r):
            product = held.tile([P, S], F32, name=f"product{b}_{r}")
            feature = x_blocks[b] if r == 0 else t[b, r]
            if r == last_term_in_psum[b]:
                nc.scalar.activation(product[:], feature[:], IDENTITY, bias=wp[:, b, :], scale=wc[:, b, r : r + 1])
            else:
                nc.scalar.activation(product[:], feature[:], COPY, scale=wc[:, b, r : r + 1])
            nc.tensor.matmul(cross_sums[b][:], identity[:], product[:], start=(r == 0), stop=(r == last_term_in_psum[b]))

        def add_to_nodew(b, r):
            nodew_next = held.tile([P, S], BF16 if r == R else F32, name=f"nodew{b}_{r}")
            nc.vector.scalar_tensor_tensor(nodew_next[:], t[b, r][:], wn[:, b, r : r + 1], nodew[b][:], MULT, ADD)
            nodew[b] = nodew_next

        add_to_cross(0, 0)
        for b in range(C_BLOCKS):
            nodew[b] = held.tile([P, S], F32, name=f"nodew{b}_0")
            nc.scalar.activation(nodew[b][:], x_blocks[b][:], COPY, scale=wn[:, b, 0:1])
        look_up(0, 1)
        add_to_cross(0, 1)
        add_to_cross(1, 0)
        look_up(1, 1)
        add_to_cross(1, 1)
        for b in range(C_BLOCKS):
            look_up(b, 2)
            add_to_cross(b, 2)
        look_up(0, 3)
        add_to_cross(0, 3)
        add_to_nodew(0, 1)
        look_up(0, 4)
        add_to_cross(0, 4)
        add_to_nodew(0, 2)
        look_up(1, 3)
        add_to_cross(1, 3)
        add_to_nodew(1, 1)
        add_to_nodew(0, 3)
        look_up(1, 4)
        add_to_nodew(1, 2)
        add_to_nodew(0, 4)
        add_to_nodew(1, 3)

        parts = [slice(0, 3 * S // 4), slice(3 * S // 4, S)]
        scores = {
            (i, h): psum.tile([P, parts[h].stop - parts[h].start], F32, name=f"scores{i}_{h}") for h in range(len(parts)) for i in range(PHRASE_BLOCKS)
        }
        for (i, h), tile in scores.items():
            nc.tensor.matmul(tile[:], ones_f32[:], constant_share[:, parts[h]], start=True, stop=False)
        p_pairs = []
        for b in range(C_BLOCKS):
            p_bf = held.tile([P, PHRASES], BF16, name=f"p_bf{b}")
            nc.scalar.copy(p_bf[:], p_f32[:, b, :])
            p_pairs.append(p_bf[:].rearrange("q (m i) -> q i m", i=PHRASE_BLOCKS))
        cross = [held.tile([P, S], BF16, name=f"cross{b}") for b in range(C_BLOCKS)]
        nc.scalar.copy(cross[0][:], cross_sums[0][:])
        add_to_nodew(1, 4)
        for part in parts:
            nc.vector.scalar_tensor_tensor(
                cross[1][:, part], t[1, R][:, part], wc[:, 1, R : R + 1], cross_sums[1][:, part], MULT, ADD
            )

        def add_to_scores(h, feature, weights, stop=False):
            for i in range(PHRASE_BLOCKS):
                nc.tensor.matmul(scores[i, h][:], weights[i], feature[:, parts[h]], start=False, stop=stop)

        all_ones = [ones[:]] * PHRASE_BLOCKS
        p_weights = [[pairs[:, i, :] for i in range(PHRASE_BLOCKS)] for pairs in p_pairs]
        result = held.tile([P, PHRASE_BLOCKS, S], F32, name="result")
        for h in range(len(parts)):
            add_to_scores(h, cross[0], p_weights[0])
        for h in range(len(parts)):
            add_to_scores(h, nodew[0], all_ones)
        for h in range(len(parts)):
            add_to_scores(h, nodew[1], all_ones)
            add_to_scores(h, cross[1], p_weights[1], stop=True)
            nc.vector.tensor_copy(result[:, 0, parts[h]], scores[0, h][:])
            nc.scalar.copy(result[:, 1, parts[h]], scores[1, h][:])
        nc.sync.dma_start(out.rearrange("(q i) s -> q i s", i=PHRASE_BLOCKS), result[:])
